import numpy as np
import ml_dtypes


def mxq(x, axis, fmt="e4m3"):
    dtype, down = {"e4m3": (ml_dtypes.float8_e4m3fn, 7), "e5m2": (ml_dtypes.float8_e5m2, 14)}[fmt]
    v = np.moveaxis(np.asarray(x, np.float32).astype(ml_dtypes.bfloat16).astype(np.float64), axis, -1)
    blocks = v.reshape(v.shape[:-1] + (-1, 32))
    amax = np.abs(blocks).max(-1, keepdims=True)
    byte = np.maximum(np.where(amax > 0, np.frexp(amax)[1] - 1 + 127, 0) - down, 1)
    scale = np.exp2(byte - 127.0)
    codes = (blocks / scale).astype(np.float32).astype(dtype).astype(np.float64)
    return np.moveaxis((codes * scale).reshape(v.shape), -1, axis)


WIDE = False


def mx_kscale(k):
    if not WIDE:
        return np.ones(k)
    levels = np.array([18, -18])
    if k % 512:
        return np.exp2(np.random.permutation(np.resize(levels, k // 32))).repeat(32)
    a = np.empty((k // 512, 16))
    for p in range(k // 512):
        a[p, :8] = np.random.permutation(np.resize(levels, 8))
        for g in range(8):
            far = levels[np.abs(levels - a[p, g]) >= 10]
            a[p, g + 8] = far[np.random.randint(len(far))]
    return np.exp2(a.ravel()).repeat(32)


BF16 = ml_dtypes.bfloat16


def bf(x):
    return np.asarray(x, np.float32).astype(BF16)


def f64(x):
    return np.asarray(x).astype(np.float64)


B, S, HID, H, HK = 2, 512, 1024, 8, 2
D = HID // H
KV = HK * D
T = B * S
J = HID + 2 * KV
THETA = 10000.0


def rope_cache():
    inv_freq = 1.0 / (THETA ** (np.arange(0, D, 2).astype(np.float64) / D))
    freqs = np.arange(S).astype(np.float64)[:, None] * inv_freq[None, :]
    emb = np.concatenate([freqs, freqs], axis=-1)
    return np.cos(emb), np.sin(emb)


def rotate_half(y):
    y1, y2 = y[..., : D // 2], y[..., D // 2 :]
    return np.concatenate([-y2, y1], axis=-1)


def to_rows(g):
    return g.transpose(0, 2, 1, 3).reshape(T, -1)


def pair_factors(u, heads):
    half = u.reshape(heads, D)[:, : D // 2]
    return np.concatenate([half, half], axis=1)


def draw_grad(heads):
    return np.random.standard_normal((B, heads, S, D)) * np.exp2(np.random.randint(-6, 1, (B, 1, S, 1)))


def setup_inputs():
    s = mx_kscale(T)
    u = mx_kscale(J)
    uq = pair_factors(u[:HID], H)
    uk = pair_factors(u[HID : HID + KV], HK)
    uv = u[HID + KV :].reshape(HK, D)
    x = bf(np.random.standard_normal((B, S, HID)) * s.reshape(B, S, 1))
    wq = bf(np.random.standard_normal((HID, HID)) * 1.4 / np.sqrt(HID) / uq.reshape(HID))
    wk = bf(np.random.standard_normal((HID, KV)) * 1.4 / np.sqrt(HID) / uk.reshape(KV))
    wv = bf(np.random.standard_normal((HID, KV)) * 2.0 / np.sqrt(HID) / uv.reshape(KV))
    st = s.reshape(B, 1, S, 1)
    g0 = bf(draw_grad(H) / st * uq[:, None, :])
    g1 = bf(draw_grad(HK) / st * uk[:, None, :])
    g2 = bf(draw_grad(HK) / st * uv[:, None, :])
    return {"hidden_states": x, "wq": wq, "wk": wk, "wv": wv, "grad_0": g0, "grad_1": g1, "grad_2": g2}


def reference(hidden_states, wq, wk, wv, grad_0, grad_1, grad_2):
    cos, sin = rope_cache()
    g0, g1, g2 = f64(grad_0), f64(grad_1), f64(grad_2)
    dq = g0 * cos - rotate_half(g0) * sin
    dk = g1 * cos - rotate_half(g1) * sin
    dz = np.concatenate([to_rows(dq), to_rows(dk), to_rows(g2)], axis=1)
    w = np.concatenate([f64(wq), f64(wk), f64(wv)], axis=1)
    x = f64(hidden_states).reshape(T, HID)
    dx = mxq(dz, 1, "e5m2") @ mxq(w, 1, "e4m3").T
    dw = mxq(x, 0, "e4m3").T @ mxq(dz, 0, "e5m2")
    return dx.reshape(B, S, HID), dw[:, :HID], dw[:, HID : HID + KV], dw[:, HID + KV :]

@@ -1,0 +1,450 @@
+import math
+from contextlib import ExitStack
+
+import concourse.mybir as mybir
+from concourse.masks import make_identity
+
+F32 = mybir.dt.float32
+BF16 = mybir.dt.bfloat16
+I32 = mybir.dt.int32
+U32 = mybir.dt.uint32
+U8 = mybir.dt.uint8
+E4M3 = mybir.dt.float8_e4m3fn_x4
+E5M2 = mybir.dt.float8_e5m2_x4
+ALU = mybir.AluOpType
+ACT = mybir.ActivationFunctionType
+
+P = 128
+B, S, HID, D = 2, 512, 1024, 128
+KV = 256
+HALF = D // 2
+THETA = 10000.0
+N = 512
+COS, SIN = 0, 1
+GB = 5
+SB = 6
+WB = 5
+PB = 6
+FLOPS = 2 * 2 * 1024 * 1024 * 1536
+
+
+def tile_multiheadattention_pa_v_kernel(
+    tc, hidden_states, wq, wk, wv, grad_0, grad_1, grad_2, out_0, out_1, out_2, out_3
+):
+    nc = tc.nc
+    V, A = nc.vector, nc.scalar
+    with ExitStack() as ctx:
+        keep = ctx.enter_context(tc.tile_pool(name="keep", bufs=1))
+        work = ctx.enter_context(tc.tile_pool(name="work", bufs=2))
+        psum = ctx.enter_context(tc.psum_pool(name="psum", bufs=1))
+        ctx.enter_context(tc.manual_schedule())
+
+        x_raw, g_raw, dz, w_raw = {}, {}, {}, {}
+        free_banks = list(range(7))
+        held, joined = {}, {}
+        prod, grouped, codes, scales, banks, staged = {}, {}, {}, {}, {}, {}
+
+        def take_bank(key, shape):
+            held[key] = free_banks[0]
+            free_banks.remove(held[key])
+            banks[key] = psum.tile(shape, F32, name=f"bank_{key}", tag=f"bank{held[key]}")
+            return banks[key]
+
+        def give_bank(key):
+            free_banks.append(held[key])
+
+        def copy_on(engine, out, in_):
+            if engine is A:
+                A.copy(out=out, in_=in_)
+            else:
+                engine.tensor_copy(out=out, in_=in_)
+
+        def load_x(b, n):
+            t = work.tile([P, 4, N], BF16, name=f"x_raw_{b}_{n}", tag="rows", bufs=4)
+            nc.sync.dma_start(
+                out=t[:], in_=hidden_states[b].rearrange("(p j) c -> p j c", j=4)[:, :, n * N : (n + 1) * N]
+            )
+            x_raw[b, n] = t
+
+        def load_g(b, g):
+            src = grad_0[b, 4 * g : 4 * g + 4] if g < 2 else grad_1[b]
+            heads = src.shape[0]
+            t = keep.tile([P, heads, 4, D], BF16, name=f"g_raw_{b}_{g}")
+            nc.sync.dma_start(out=t[:], in_=src.rearrange("h (p j) d -> p h j d", j=4))
+            g_raw[b, g] = t
+
+        def load_v(b):
+            t = keep.tile([P, 4, N], BF16, name=f"dz_{b}_2")
+            for h in range(2):
+                nc.sync.dma_start(
+                    out=t[:, :, KV + h * D : KV + (h + 1) * D],
+                    in_=grad_2[b, h].rearrange("(p j) d -> p j d", j=4),
+                )
+            dz[b, 2] = t
+
+        def load_wq(n):
+            t = keep.tile([P, 4, HID], BF16, name=f"wq_raw_{n}")
+            nc.sync.dma_start(out=t[:], in_=wq[n * N : (n + 1) * N, :].rearrange("(i p) k -> p i k", p=P))
+            w_raw[0, n] = t[:, :, 0:N]
+            w_raw[1, n] = t[:, :, N:HID]
+
+        def load_wkv(n):
+            t = keep.tile([P, 4, N], BF16, name=f"wkv_raw_{n}")
+            rows = slice(n * N, (n + 1) * N)
+            nc.sync.dma_start(out=t[:, :, 0:KV], in_=wk[rows, :].rearrange("(i p) k -> p i k", p=P))
+            nc.sync.dma_start(out=t[:, :, KV:N], in_=wv[rows, :].rearrange("(i p) k -> p i k", p=P))
+            w_raw[2, n] = t[:]
+
+        def interleave(engine, key, src, part=0, parts=1):
+            cols = slice(part * N // parts, (part + 1) * N // parts)
+            copy_on(
+                engine,
+                grouped[key][:, cols, :].rearrange("p (c i) j -> p c j i", i=4),
+                src[:, :, cols].rearrange("p j (c i) -> p c j i", i=4),
+            )
+
+        def operands(*keys):
+            name = "_".join(keys)
+            width = N * len(keys)
+            joined[keys] = (
+                work.tile([P, width, 4], BF16, name=f"grouped_{name}", tag="grouped", bufs=GB, align_bytes=64),
+                keep.tile([P, width], U32, name=f"code_{name}", align_bytes=64),
+                keep.tile([P, width], U8, name=f"scale_{name}", align_bytes=64),
+            )
+            for k, key in enumerate(keys):
+                cols = slice(k * N, (k + 1) * N)
+                grouped[key] = joined[keys][0][:, cols, :]
+                codes[key] = joined[keys][1][:, cols]
+                scales[key] = joined[keys][2][:, cols]
+
+        def quantize(keys, fmt, part=0, parts=1):
+            values, code, scale = joined[keys]
+            width = N * len(keys) // parts
+            cols = slice(part * width, (part + 1) * width)
+            V.quantize_mx(
+                out=code[:, cols].bitcast(fmt),
+                scales=scale[:, cols],
+                in_=values[:, cols, :].rearrange("p c j -> p (c j)"),
+            )
+
+        def turn(key, src, pair):
+            bank = take_bank(f"{key}_{pair}", [P, 2, 2, P])
+            words = src.bitcast(F32)
+            for r in range(2):
+                for u in range(2):
+                    nc.tensor.transpose(bank[:, r, u, :], words[:, 2 * pair + r, u : N // 2 : 2], ident[:])
+
+        def turn_out(engine, key, pair):
+            words = grouped[key].rearrange("p c t -> p (c t)").bitcast(F32)
+            copy_on(
+                engine,
+                words[:, pair * N : (pair + 1) * N].rearrange("p (r c u) -> p r c u", r=2, u=2),
+                banks[f"{key}_{pair}"][:].rearrange("p r u c -> p r c u"),
+            )
+            give_bank(f"{key}_{pair}")
+
+        def multiply(which, b, g, s, rows=slice(0, 4)):
+            heads = g_raw[b, g].shape[1]
+            if rows.start == 0:
+                prod[which, b, g, s] = work.tile(
+                    [P, heads, 4, HALF], F32, name=f"prod_{which}_{b}_{g}_{s}", tag="prod", bufs=PB
+                )
+            count = rows.stop - rows.start
+            V.tensor_tensor(
+                out=prod[which, b, g, s][:, :, rows],
+                in0=g_raw[b, g][:, :, rows, s * HALF : (s + 1) * HALF],
+                in1=trig[:, rows, which * HALF : (which + 1) * HALF].unsqueeze(1).to_broadcast([P, heads, count, HALF]),
+                op=ALU.mult,
+            )
+
+        def rotate(engine, b, g, s, rows=slice(0, 4)):
+            heads = g_raw[b, g].shape[1]
+            if (b, g) not in dz:
+                dz[b, g] = work.tile([P, 4, N], BF16, name=f"dz_{b}_{g}", tag="rows", bufs=4)
+            engine.tensor_tensor(
+                out=dz[b, g][:].rearrange("p j (h s d) -> p s h j d", s=2, d=HALF)[:, s, 0:heads, rows],
+                in0=prod[COS, b, g, s][:, :, rows],
+                in1=prod[SIN, b, g, 1 - s][:, :, rows],
+                op=ALU.add if s == 0 else ALU.subtract,
+            )
+
+        def mm(acc, lhs, m, rhs, start, stop, lhs_fmt, rhs_fmt):
+            cols = slice(m * P, (m + 1) * P)
+            nc.tensor.matmul_mx(
+                out=acc[:],
+                lhsT=codes[lhs][:, cols].bitcast(lhs_fmt),
+                lhsT_scale=scales[lhs][:, cols],
+                rhs=codes[rhs].bitcast(rhs_fmt),
+                rhs_scale=scales[rhs],
+                start=start,
+                stop=stop,
+            )
+
+        def dx_pass(b, j, n, g, first, last):
+            if first:
+                take_bank(f"dx{b}{j}{n}", [P, N])
+            mm(banks[f"dx{b}{j}{n}"], f"zf{b}{g}", j, f"w{g}{n}", first, last, E5M2, E4M3)
+
+        def dx_out(engine, b, j, n):
+            t = work.tile([P, N], F32, name=f"dx_rows_{b}_{j}_{n}", tag="dx_staged", bufs=SB)
+            copy_on(engine, t[:], banks[f"dx{b}{j}{n}"][:])
+            give_bank(f"dx{b}{j}{n}")
+            nc.sync.dma_start(out=out_0[b].rearrange("(p j) c -> p j c", j=4)[:, j, n * N : (n + 1) * N], in_=t[:])
+
+        def dw_pass(i, g, b):
+            if b == 0:
+                take_bank(f"dw{i}{g}", [P, N])
+            mm(banks[f"dw{i}{g}"], f"x{b}{i // 4}", i % 4, f"zt{b}{g}", b == 0, b == 1, E4M3, E5M2)
+
+        def dw_out(engine, i, g):
+            if i % 2 == 0:
+                staged["dw", i // 2, g] = work.tile([P, HID], F32, name=f"dw_rows_{i}_{g}", tag="dw_staged", bufs=WB)
+            t = staged["dw", i // 2, g][:].rearrange("p (i c) -> p i c", i=2)
+            copy_on(engine, t[:, i % 2, :], banks[f"dw{i}{g}"][:])
+            give_bank(f"dw{i}{g}")
+            if i % 2 == 1:
+                rows = slice((i - 1) * P, (i + 1) * P)
+                if g < 2:
+                    nc.sync.dma_start(
+                        out=out_1[rows, g * N : (g + 1) * N].rearrange("(i p) c -> p i c", p=P), in_=t
+                    )
+                else:
+                    nc.sync.dma_start(out=out_2[rows, :].rearrange("(i p) c -> p i c", p=P), in_=t[:, :, 0:KV])
+                    nc.sync.dma_start(out=out_3[rows, :].rearrange("(i p) c -> p i c", p=P), in_=t[:, :, KV:N])
+
+
+        G = nc.gpsimd
+        load_x(0, 0)
+        load_x(1, 0)
+        load_g(0, 2)
+        load_g(1, 2)
+        load_x(0, 1)
+        load_v(0)
+        load_v(1)
+        load_x(1, 1)
+        load_g(0, 0)
+        load_wkv(0)
+        load_wq(0)
+        load_g(0, 1)
+        load_wkv(1)
+        load_wq(1)
+        load_g(1, 0)
+        load_g(1, 1)
+
+        warm = keep.tile([P, 1], F32, name="warm")
+        zero_one = keep.tile([P, 2], F32, name="zero_one")
+        ident = keep.tile([P, P], F32, name="ident")
+        position = keep.tile([P, 4, P], F32, name="position")
+        coarse = keep.tile([P, 8], F32, name="coarse")
+        fine = keep.tile([P, 8], F32, name="fine")
+        quarter = keep.tile([P, 1], F32, name="quarter")
+        phase = keep.tile([P, 1], F32, name="phase")
+        freq_row = keep.tile([P, 2, 8, 8], F32, name="freq_row")
+        freq_diag = keep.tile([P, P], F32, name="freq_diag")
+        freq = keep.tile([P, 1], F32, name="freq")
+        whole = keep.tile([P, S], I32, name="whole")
+        rest = keep.tile([P, S], F32, name="rest")
+        trig_t = keep.tile([P, 4, P], F32, name="trig_t")
+        trig = psum.tile([P, 4, P], F32, name="trig")
+
+        V.memset(zero_one[:, 0:1], 0.0)
+        V.memset(zero_one[:, 1:2], 1.0)
+        make_identity(nc, ident[:])
+        nc.gpsimd.iota(
+            position[:], [[1, 4], [4, P]], base=0, channel_multiplier=0, allow_small_or_imprecise_dtypes=True
+        )
+        V.memset(quarter[0:HALF, :], 0.25)
+        V.memset(quarter[HALF:P, :], 0.0)
+        A.activation(out=warm[:], in_=zero_one[:, 0:1], func=ACT.Sin)
+        for a in range(0, 8, 2):
+            lo, hi = (THETA ** (-8 * e / HALF) / (2 * math.pi) for e in (a, a + 1))
+            V.tensor_scalar(
+                out=coarse[:, a : a + 2], in0=zero_one[:], scalar1=hi - lo, scalar2=lo, op0=ALU.mult, op1=ALU.add
+            )
+            lo, hi = (THETA ** (-e / HALF) for e in (a, a + 1))
+            V.tensor_scalar(
+                out=fine[:, a : a + 2], in0=zero_one[:], scalar1=hi - lo, scalar2=lo, op0=ALU.mult, op1=ALU.add
+            )
+        V.tensor_scalar(out=phase[:], in0=quarter[:], scalar1=2 * math.pi, scalar2=None, op0=ALU.mult)
+        V.tensor_tensor(
+            out=freq_row[:],
+            in0=coarse[:].unsqueeze(1).unsqueeze(3).to_broadcast([P, 2, 8, 8]),
+            in1=fine[:].unsqueeze(1).unsqueeze(1).to_broadcast([P, 2, 8, 8]),
+            op=ALU.mult,
+        )
+        V.scalar_tensor_tensor(
+            out=freq_diag[:],
+            in0=freq_row[:].rearrange("p s a b -> p (s a b)"),
+            scalar=1.0,
+            in1=ident[:],
+            op0=ALU.mult,
+            op1=ALU.mult,
+            accum_out=freq[:],
+        )
+        flat_position = position[:].rearrange("p j r -> p (j r)")
+        V.tensor_scalar(
+            out=whole[:], in0=flat_position, scalar1=freq[:], scalar2=quarter[:], op0=ALU.mult, op1=ALU.add
+        )
+        V.scalar_tensor_tensor(
+            out=rest[:], in0=flat_position, scalar=freq[:], in1=whole[:], op0=ALU.mult, op1=ALU.subtract
+        )
+        A.activation(
+            out=trig_t[:].rearrange("p j r -> p (j r)"), in_=rest[:], func=ACT.Sin, bias=phase[:], scale=2 * math.pi
+        )
+        for j in range(4):
+            nc.tensor.transpose(trig[:, j, :], trig_t[:, j, :], ident[:])
+
+
+        LO, HI = slice(0, 2), slice(2, 4)
+
+        def turns(key, src):
+            turn(key, src, 0)
+            turn(key, src, 1)
+
+        def turns_out(key, e0=A, e1=A):
+            turn_out(e0, key, 0)
+            turn_out(e1, key, 1)
+
+        def dw_mm(i, g):
+            dw_pass(i, g, 0)
+            dw_pass(i, g, 1)
+
+        def products(b, g, s, rows=slice(0, 4)):
+            multiply(COS, b, g, s, rows)
+            multiply(SIN, b, g, 1 - s, rows)
+
+        def dx_mm(b, j, n, passes):
+            for g in passes:
+                dx_pass(b, j, n, g, g == 2, g == 1)
+
+        operands("x00")
+        operands("x10")
+        operands("x01", "x11")
+        operands("zt02", "zt12")
+        interleave(V, "x00", x_raw[0, 0][:])
+        quantize(("x00",), E4M3)
+        interleave(A, "x10", x_raw[1, 0][:])
+        interleave(A, "x01", x_raw[0, 1][:])
+        products(0, 2, 0)
+        rotate(G, 0, 2, 0)
+        products(0, 2, 1)
+        quantize(("x10",), E4M3)
+        rotate(G, 0, 2, 1)
+        products(1, 2, 0)
+        rotate(G, 1, 2, 0)
+        products(1, 2, 1)
+        interleave(A, "zt02", dz[0, 2][:])
+        multiply(COS, 0, 0, 0)
+        rotate(V, 1, 2, 1)
+        interleave(A, "x11", x_raw[1, 1][:])
+        multiply(SIN, 0, 0, 1)
+        interleave(V, "zt12", dz[1, 2][:])
+        rotate(G, 0, 0, 0)
+        operands("w20", "w00")
+        turns("w20", w_raw[2, 0])
+        turns("zf02", dz[0, 2][:])
+        multiply(COS, 0, 0, 1)
+        multiply(SIN, 0, 0, 0)
+        quantize(("zt02", "zt12"), E5M2)
+        rotate(G, 0, 0, 1)
+        turns_out("w20")
+        turns("w00", w_raw[0, 0])
+        operands("zf02", "zf00")
+        turns_out("zf02")
+        for i in range(3):
+            dw_mm(i, 2)
+        turns_out("w00")
+        products(0, 1, 0)
+        quantize(("x01", "x11"), E4M3)
+        rotate(G, 0, 1, 0)
+        dw_mm(3, 2)
+        turns("w10", w_raw[1, 0])
+        for i in range(4):
+            dw_out(A, i, 2)
+        operands("w10", "w21")
+        turns("zf00", dz[0, 0][:])
+        turns_out("w10")
+        for i in range(4, 7):
+            dw_mm(i, 2)
+        turns_out("zf00")
+        products(0, 1, 1)
+        quantize(("w20", "w00"), E4M3)
+        rotate(G, 0, 1, 1)
+        dw_mm(7, 2)
+        turns("w21", w_raw[2, 1])
+        for i in range(4, 8):
+            dw_out(A, i, 2)
+        turns("w01", w_raw[0, 1])
+        turns_out("w21")
+        products(1, 0, 0)
+        quantize(("zf02", "zf00"), E5M2)
+        rotate(G, 1, 0, 0)
+        operands("w01", "w11")
+        turns("zf01", dz[0, 1][:])
+        turns_out("w01")
+        turns("w11", w_raw[1, 1])
+        operands("zf01")
+        turns_out("zf01")
+        for j in range(3):
+            dx_mm(0, j, 0, (2, 0))
+        turns_out("w11")
+        products(1, 0, 1)
+        quantize(("w10", "w21"), E4M3)
+        quantize(("zf01",), E5M2)
+        operands("zt00", "zt10")
+        interleave(A, "zt00", dz[0, 0][:])
+        dx_mm(0, 3, 0, (2, 0))
+        for j in range(4):
+            dx_mm(0, j, 0, (1,))
+        rotate(V, 1, 0, 1)
+        quantize(("w01", "w11"), E4M3)
+        interleave(V, "zt10", dz[1, 0][:])
+        turns("zf12", dz[1, 2][:])
+        for j in range(4):
+            dx_out(A, 0, j, 0)
+        operands("zf12", "zf10")
+        for j in range(2):
+            dx_mm(0, j, 1, (2, 0, 1))
+        turns_out("zf12")
+        turns("zf10", dz[1, 0][:])
+        multiply(COS, 1, 1, 0)
+        quantize(("zt00", "zt10"), E5M2)
+        for j in range(2, 4):
+            dx_mm(0, j, 1, (2, 0, 1))
+        for j in range(2):
+            dx_out(A, 0, j, 1)
+        turns_out("zf10")
+        for j in range(2, 4):
+            dx_out(A, 0, j, 1)
+        multiply(SIN, 1, 1, 1)
+        rotate(G, 1, 1, 0)
+        operands("zt01", "zt11")
+        operands("zf11")
+        for i in range(4):
+            dw_mm(i, 0)
+        products(1, 1, 1)
+        quantize(("zf12", "zf10"), E5M2)
+        interleave(A, "zt01", dz[0, 1][:])
+        rotate(V, 1, 1, 1, LO)
+        rotate(V, 1, 1, 1, HI)
+        for i in range(4):
+            dw_out(A, i, 0)
+        for i in range(4, 6):
+            dw_mm(i, 0)
+        turns("zf11", dz[1, 1][:])
+        for i in range(6, 8):
+            dw_mm(i, 0)
+        interleave(V, "zt11", dz[1, 1][:])
+        turn_out(V, "zf11", 0)
+        turn_out(A, "zf11", 1)
+        for i in range(4, 8):
+            dw_out(A, i, 0)
+        quantize(("zt01", "zt11"), E5M2)
+        quantize(("zf11",), E5M2)
+        for j in range(4):
+            for n in range(2):
+                dx_mm(1, j, n, (2, 0, 1))
+                dx_out((A, V)[n], 1, j, n)
+        for i in range(8):
+            dw_mm(i, 1)
+            dw_out((A, V)[i % 2], i, 1)

@@ -16,84 +16,144 @@ ACT = mybir.ActivationFunctionType
 
 P = 128
 B, S, HID, D = 2, 512, 1024, 128
-KV = 256
+KV_WIDTH = 256
 HALF = D // 2
 THETA = 10000.0
 N = 512
+PACK = 4
+Q_LO, Q_HI, KV = 0, 1, 2
 COS, SIN = 0, 1
-GB = 5
-SB = 6
-WB = 5
-PB = 6
-FLOPS = 2 * 2 * 1024 * 1024 * 1536
+ALL_ROWS, FIRST_ROWS, LAST_ROWS = slice(0, 4), slice(0, 2), slice(2, 4)
+
+WORK_BANKS = 7
+SINGLE_SLOTS, PAIR_SLOTS = 3, 5
+PRODUCT_BUFS = 9
+BANK_STAGING_BUFS = 5
+DZ_PLACE = {(0, Q_LO): "v_raw", (0, Q_HI): "k_raw", (1, Q_LO): "wkv_0", (1, Q_HI): "q_0_0"}
+TWO_BANK_STAGING_PLACES = ("x_0", "x_1", "wkv_1", "q_0_1", "wq_0", "wq_1")
+
+FLOPS = 2 * 2 * (B * S) * HID * (HID + 2 * KV_WIDTH)
+
+
+def x_op(b, n):
+    return f"x{b}{n}"
+
+
+def w_op(g, n):
+    return f"w{g}{n}"
+
+
+def dz_tok(b, g):
+    return f"zt{b}{g}"
+
+
+def dz_feat(b, g):
+    return f"zf{b}{g}"
 
 
 def tile_multiheadattention_pa_v_kernel(
     tc, hidden_states, wq, wk, wv, grad_0, grad_1, grad_2, out_0, out_1, out_2, out_3
 ):
     nc = tc.nc
-    V, A = nc.vector, nc.scalar
+    vector, scalar, gpsimd = nc.vector, nc.scalar, nc.gpsimd
     with ExitStack() as ctx:
         keep = ctx.enter_context(tc.tile_pool(name="keep", bufs=1))
-        work = ctx.enter_context(tc.tile_pool(name="work", bufs=2))
+        work = ctx.enter_context(tc.tile_pool(name="work", bufs=1))
         psum = ctx.enter_context(tc.psum_pool(name="psum", bufs=1))
         ctx.enter_context(tc.manual_schedule())
 
-        x_raw, g_raw, dz, w_raw = {}, {}, {}, {}
-        free_banks = list(range(7))
-        held, joined = {}, {}
-        prod, grouped, codes, scales, banks, staged = {}, {}, {}, {}, {}, {}
+        x_raw, w_raw, grad_raw, dz, product = {}, {}, {}, {}, {}
+        grouped, codes, scales, together, slot_of = {}, {}, {}, {}, {}
+        banks, bank_number, staged = {}, {}, {}
+        free_banks = list(range(WORK_BANKS))
+        free_slots = {1: list(range(SINGLE_SLOTS)), 2: list(range(PAIR_SLOTS))}
+        staging_places = list(TWO_BANK_STAGING_PLACES)
+
 
         def take_bank(key, shape):
-            held[key] = free_banks[0]
-            free_banks.remove(held[key])
-            banks[key] = psum.tile(shape, F32, name=f"bank_{key}", tag=f"bank{held[key]}")
+            bank_number[key] = free_banks[0]
+            free_banks.remove(bank_number[key])
+            banks[key] = psum.tile(shape, F32, name=f"bank_{key}", tag=f"bank{bank_number[key]}")
             return banks[key]
 
         def give_bank(key):
-            free_banks.append(held[key])
+            free_banks.append(bank_number[key])
+
+        def next_staging_place():
+            place = staging_places[0]
+            staging_places.remove(place)
+            staging_places.append(place)
+            return place
 
         def copy_on(engine, out, in_):
-            if engine is A:
-                A.copy(out=out, in_=in_)
+            if engine is scalar:
+                scalar.copy(out=out, in_=in_)
             else:
-                engine.tensor_copy(out=out, in_=in_)
+                vector.tensor_copy(out=out, in_=in_)
 
-        def load_x(b, n):
-            t = work.tile([P, 4, N], BF16, name=f"x_raw_{b}_{n}", tag="rows", bufs=4)
+
+        def load_x(b):
+            tile = keep.tile([P, PACK, HID], BF16, name=f"x_raw_{b}", tag=f"x_{b}")
+            nc.sync.dma_start(out=tile[:], in_=hidden_states[b].rearrange("(p j) c -> p j c", j=PACK))
+            for n in range(2):
+                x_raw[b, n] = tile[:, :, n * N : (n + 1) * N]
+
+        def load_q(b, g):
+            tile = keep.tile([P, 4, PACK, D], BF16, name=f"q_raw_{b}_{g}", tag=f"q_{b}_{g}")
+            heads = grad_0[b, 4 * g : 4 * g + 4]
+            nc.sync.dma_start(out=tile[:], in_=heads.rearrange("h (p j) d -> p h j d", j=PACK))
+            grad_raw[b, g] = tile[:]
+
+        def load_two_heads(grad, name):
+            tile = keep.tile([P, B, 2, PACK, D], BF16, name=name, tag=name)
             nc.sync.dma_start(
-                out=t[:], in_=hidden_states[b].rearrange("(p j) c -> p j c", j=4)[:, :, n * N : (n + 1) * N]
+                out=tile[:].rearrange("p b h j d -> p (b h) (j d)"),
+                in_=grad.rearrange("b h (p j) d -> p (b h) (j d)", j=PACK),
             )
-            x_raw[b, n] = t
-
-        def load_g(b, g):
-            src = grad_0[b, 4 * g : 4 * g + 4] if g < 2 else grad_1[b]
-            heads = src.shape[0]
-            t = keep.tile([P, heads, 4, D], BF16, name=f"g_raw_{b}_{g}")
-            nc.sync.dma_start(out=t[:], in_=src.rearrange("h (p j) d -> p h j d", j=4))
-            g_raw[b, g] = t
-
-        def load_v(b):
-            t = keep.tile([P, 4, N], BF16, name=f"dz_{b}_2")
-            for h in range(2):
-                nc.sync.dma_start(
-                    out=t[:, :, KV + h * D : KV + (h + 1) * D],
-                    in_=grad_2[b, h].rearrange("(p j) d -> p j d", j=4),
-                )
-            dz[b, 2] = t
+            return tile
 
         def load_wq(n):
-            t = keep.tile([P, 4, HID], BF16, name=f"wq_raw_{n}")
-            nc.sync.dma_start(out=t[:], in_=wq[n * N : (n + 1) * N, :].rearrange("(i p) k -> p i k", p=P))
-            w_raw[0, n] = t[:, :, 0:N]
-            w_raw[1, n] = t[:, :, N:HID]
+            tile = keep.tile([P, 4, HID], BF16, name=f"wq_raw_{n}", tag=f"wq_{n}")
+            nc.sync.dma_start(out=tile[:], in_=wq[n * N : (n + 1) * N, :].rearrange("(i p) k -> p i k", p=P))
+            w_raw[Q_LO, n] = tile[:, :, 0:N]
+            w_raw[Q_HI, n] = tile[:, :, N:HID]
 
         def load_wkv(n):
-            t = keep.tile([P, 4, N], BF16, name=f"wkv_raw_{n}")
+            tile = keep.tile([P, 4, N], BF16, name=f"wkv_raw_{n}", tag=f"wkv_{n}")
             rows = slice(n * N, (n + 1) * N)
-            nc.sync.dma_start(out=t[:, :, 0:KV], in_=wk[rows, :].rearrange("(i p) k -> p i k", p=P))
-            nc.sync.dma_start(out=t[:, :, KV:N], in_=wv[rows, :].rearrange("(i p) k -> p i k", p=P))
-            w_raw[2, n] = t[:]
+            nc.sync.dma_start(out=tile[:, :, 0:KV_WIDTH], in_=wk[rows, :].rearrange("(i p) k -> p i k", p=P))
+            nc.sync.dma_start(out=tile[:, :, KV_WIDTH:N], in_=wv[rows, :].rearrange("(i p) k -> p i k", p=P))
+            w_raw[KV, n] = tile[:]
+
+
+        def operands(*keys):
+            name = "_".join(keys)
+            width = N * len(keys)
+            slot_of[keys] = free_slots[len(keys)][0]
+            free_slots[len(keys)].remove(slot_of[keys])
+            tag = f"grouped_{len(keys)}_{slot_of[keys]}"
+            together[keys] = (
+                work.tile([P, width, PACK], BF16, name=f"grouped_{name}", tag=tag, align_bytes=64),
+                keep.tile([P, width], U32, name=f"code_{name}", align_bytes=64),
+                keep.tile([P, width], U8, name=f"scale_{name}", align_bytes=64),
+            )
+            for k, key in enumerate(keys):
+                cols = slice(k * N, (k + 1) * N)
+                grouped[key] = together[keys][0][:, cols, :]
+                codes[key] = together[keys][1][:, cols]
+                scales[key] = together[keys][2][:, cols]
+
+        def quantize(keys, fmt, part=0, parts=1):
+            values, code, scale = together[keys]
+            width = N * len(keys) // parts
+            cols = slice(part * width, (part + 1) * width)
+            vector.quantize_mx(
+                out=code[:, cols].bitcast(fmt),
+                scales=scale[:, cols],
+                in_=values[:, cols, :].rearrange("p c j -> p (c j)"),
+            )
+            if part == parts - 1:
+                free_slots[len(keys)].append(slot_of[keys])
 
         def interleave(engine, key, src, part=0, parts=1):
             cols = slice(part * N // parts, (part + 1) * N // parts)
@@ -101,30 +161,6 @@ def tile_multiheadattention_pa_v_kernel(
                 engine,
                 grouped[key][:, cols, :].rearrange("p (c i) j -> p c j i", i=4),
                 src[:, :, cols].rearrange("p j (c i) -> p c j i", i=4),
-            )
-
-        def operands(*keys):
-            name = "_".join(keys)
-            width = N * len(keys)
-            joined[keys] = (
-                work.tile([P, width, 4], BF16, name=f"grouped_{name}", tag="grouped", bufs=GB, align_bytes=64),
-                keep.tile([P, width], U32, name=f"code_{name}", align_bytes=64),
-                keep.tile([P, width], U8, name=f"scale_{name}", align_bytes=64),
-            )
-            for k, key in enumerate(keys):
-                cols = slice(k * N, (k + 1) * N)
-                grouped[key] = joined[keys][0][:, cols, :]
-                codes[key] = joined[keys][1][:, cols]
-                scales[key] = joined[keys][2][:, cols]
-
-        def quantize(keys, fmt, part=0, parts=1):
-            values, code, scale = joined[keys]
-            width = N * len(keys) // parts
-            cols = slice(part * width, (part + 1) * width)
-            V.quantize_mx(
-                out=code[:, cols].bitcast(fmt),
-                scales=scale[:, cols],
-                in_=values[:, cols, :].rearrange("p c j -> p (c j)"),
             )
 
         def turn(key, src, pair):
@@ -143,32 +179,51 @@ def tile_multiheadattention_pa_v_kernel(
             )
             give_bank(f"{key}_{pair}")
 
-        def multiply(which, b, g, s, rows=slice(0, 4)):
-            heads = g_raw[b, g].shape[1]
+        def turns(key, src):
+            for pair in range(2):
+                turn(key, src, pair)
+
+        def turns_out(key):
+            for pair in range(2):
+                turn_out(scalar, key, pair)
+
+
+        def multiply(which, b, g, half, rows=ALL_ROWS):
+            heads = grad_raw[b, g].shape[1]
             if rows.start == 0:
-                prod[which, b, g, s] = work.tile(
-                    [P, heads, 4, HALF], F32, name=f"prod_{which}_{b}_{g}_{s}", tag="prod", bufs=PB
+                product[which, b, g, half] = work.tile(
+                    [P, heads, PACK, HALF],
+                    F32,
+                    name=f"prod_{which}_{b}_{g}_{half}",
+                    tag="product",
+                    bufs=PRODUCT_BUFS,
                 )
-            count = rows.stop - rows.start
-            V.tensor_tensor(
-                out=prod[which, b, g, s][:, :, rows],
-                in0=g_raw[b, g][:, :, rows, s * HALF : (s + 1) * HALF],
-                in1=trig[:, rows, which * HALF : (which + 1) * HALF].unsqueeze(1).to_broadcast([P, heads, count, HALF]),
+            table = trig[:, rows, which * HALF : (which + 1) * HALF]
+            vector.tensor_tensor(
+                out=product[which, b, g, half][:, :, rows],
+                in0=grad_raw[b, g][:, :, rows, half * HALF : (half + 1) * HALF],
+                in1=table.unsqueeze(1).to_broadcast([P, heads, rows.stop - rows.start, HALF]),
                 op=ALU.mult,
             )
 
-        def rotate(engine, b, g, s, rows=slice(0, 4)):
-            heads = g_raw[b, g].shape[1]
+        def products(b, g, half, rows=ALL_ROWS):
+            multiply(COS, b, g, half, rows)
+            multiply(SIN, b, g, 1 - half, rows)
+
+        def combine(engine, b, g, half, rows=ALL_ROWS):
+            heads = grad_raw[b, g].shape[1]
             if (b, g) not in dz:
-                dz[b, g] = work.tile([P, 4, N], BF16, name=f"dz_{b}_{g}", tag="rows", bufs=4)
+                tile = keep.tile([P, PACK, N], BF16, name=f"dz_{b}_{g}", tag=DZ_PLACE[b, g])
+                dz[b, g] = tile[:]
             engine.tensor_tensor(
-                out=dz[b, g][:].rearrange("p j (h s d) -> p s h j d", s=2, d=HALF)[:, s, 0:heads, rows],
-                in0=prod[COS, b, g, s][:, :, rows],
-                in1=prod[SIN, b, g, 1 - s][:, :, rows],
-                op=ALU.add if s == 0 else ALU.subtract,
+                out=dz[b, g].rearrange("p j (h s d) -> p s h j d", s=2, d=HALF)[:, half, 0:heads, rows],
+                in0=product[COS, b, g, half][:, :, rows],
+                in1=product[SIN, b, g, 1 - half][:, :, rows],
+                op=ALU.add if half == 0 else ALU.subtract,
             )
 
-        def mm(acc, lhs, m, rhs, start, stop, lhs_fmt, rhs_fmt):
+
+        def matmul(acc, lhs, m, rhs, start, stop, lhs_fmt, rhs_fmt):
             cols = slice(m * P, (m + 1) * P)
             nc.tensor.matmul_mx(
                 out=acc[:],
@@ -180,101 +235,112 @@ def tile_multiheadattention_pa_v_kernel(
                 stop=stop,
             )
 
-        def dx_pass(b, j, n, g, first, last):
-            if first:
-                take_bank(f"dx{b}{j}{n}", [P, N])
-            mm(banks[f"dx{b}{j}{n}"], f"zf{b}{g}", j, f"w{g}{n}", first, last, E5M2, E4M3)
+        def dx_matmuls(b, j, n, groups=(KV, Q_LO, Q_HI)):
+            key = f"dx{b}{j}{n}"
+            for g in groups:
+                if g == KV:
+                    take_bank(key, [P, N])
+                matmul(banks[key], dz_feat(b, g), j, w_op(g, n), g == KV, g == Q_HI, E5M2, E4M3)
 
-        def dx_out(engine, b, j, n):
-            t = work.tile([P, N], F32, name=f"dx_rows_{b}_{j}_{n}", tag="dx_staged", bufs=SB)
-            copy_on(engine, t[:], banks[f"dx{b}{j}{n}"][:])
-            give_bank(f"dx{b}{j}{n}")
-            nc.sync.dma_start(out=out_0[b].rearrange("(p j) c -> p j c", j=4)[:, j, n * N : (n + 1) * N], in_=t[:])
+        def dx_out(engine, b, j, n, whole_rows=False):
+            key = f"dx{b}{j}{n}"
+            rows = out_0[b].rearrange("(p j) c -> p j c", j=PACK)[:, j, :]
+            cols = slice(n * N, (n + 1) * N)
+            if not whole_rows:
+                tile = work.tile([P, N], F32, name=f"dx_rows_{b}_{j}_{n}", tag="staged", bufs=BANK_STAGING_BUFS)
+                copy_on(engine, tile[:], banks[key][:])
+                nc.sync.dma_start(out=rows[:, cols], in_=tile[:])
+            else:
+                if n == 0:
+                    staged["dx"] = keep.tile([P, HID], F32, name=f"dx_rows_{b}_{j}", tag=next_staging_place())
+                copy_on(engine, staged["dx"][:, cols], banks[key][:])
+                if n == 1:
+                    nc.sync.dma_start(out=rows, in_=staged["dx"][:])
+            give_bank(key)
 
-        def dw_pass(i, g, b):
-            if b == 0:
-                take_bank(f"dw{i}{g}", [P, N])
-            mm(banks[f"dw{i}{g}"], f"x{b}{i // 4}", i % 4, f"zt{b}{g}", b == 0, b == 1, E4M3, E5M2)
+        def dw_matmuls(i, g):
+            acc = take_bank(f"dw{i}{g}", [P, N])
+            for b in range(B):
+                matmul(acc, x_op(b, i // 4), i % 4, dz_tok(b, g), b == 0, b == B - 1, E4M3, E5M2)
 
         def dw_out(engine, i, g):
             if i % 2 == 0:
-                staged["dw", i // 2, g] = work.tile([P, HID], F32, name=f"dw_rows_{i}_{g}", tag="dw_staged", bufs=WB)
-            t = staged["dw", i // 2, g][:].rearrange("p (i c) -> p i c", i=2)
-            copy_on(engine, t[:, i % 2, :], banks[f"dw{i}{g}"][:])
+                staged["dw"] = keep.tile([P, 2, N], F32, name=f"dw_rows_{i}_{g}", tag=next_staging_place())
+            tile = staged["dw"]
+            copy_on(engine, tile[:, i % 2, :], banks[f"dw{i}{g}"][:])
             give_bank(f"dw{i}{g}")
             if i % 2 == 1:
                 rows = slice((i - 1) * P, (i + 1) * P)
-                if g < 2:
-                    nc.sync.dma_start(
-                        out=out_1[rows, g * N : (g + 1) * N].rearrange("(i p) c -> p i c", p=P), in_=t
-                    )
+                if g == KV:
+                    for out, cols in ((out_2, slice(0, KV_WIDTH)), (out_3, slice(KV_WIDTH, N))):
+                        nc.sync.dma_start(out=out[rows, :].rearrange("(i p) c -> p i c", p=P), in_=tile[:, :, cols])
                 else:
-                    nc.sync.dma_start(out=out_2[rows, :].rearrange("(i p) c -> p i c", p=P), in_=t[:, :, 0:KV])
-                    nc.sync.dma_start(out=out_3[rows, :].rearrange("(i p) c -> p i c", p=P), in_=t[:, :, KV:N])
+                    dest = out_1[rows, g * N : (g + 1) * N]
+                    nc.sync.dma_start(out=dest.rearrange("(i p) c -> p i c", p=P), in_=tile[:])
 
-
-        G = nc.gpsimd
-        load_x(0, 0)
-        load_x(1, 0)
-        load_g(0, 2)
-        load_g(1, 2)
-        load_x(0, 1)
-        load_v(0)
-        load_v(1)
-        load_x(1, 1)
-        load_g(0, 0)
+        load_x(0)
+        k_raw = load_two_heads(grad_1, "k_raw")
+        load_x(1)
+        v_raw = load_two_heads(grad_2, "v_raw")
+        load_q(0, Q_LO)
         load_wkv(0)
         load_wq(0)
-        load_g(0, 1)
+        load_q(0, Q_HI)
         load_wkv(1)
         load_wq(1)
-        load_g(1, 0)
-        load_g(1, 1)
+        load_q(1, Q_LO)
+        load_q(1, Q_HI)
+        dz_kv = keep.tile([P, B, PACK, N], BF16, name="dz_kv")
+        for b in range(B):
+            grad_raw[b, KV] = k_raw[:, b]
+            dz[b, KV] = dz_kv[:, b]
 
-        warm = keep.tile([P, 1], F32, name="warm")
         zero_one = keep.tile([P, 2], F32, name="zero_one")
         ident = keep.tile([P, P], F32, name="ident")
-        position = keep.tile([P, 4, P], F32, name="position")
+        position = keep.tile([P, PACK, P], F32, name="position")
         coarse = keep.tile([P, 8], F32, name="coarse")
         fine = keep.tile([P, 8], F32, name="fine")
         quarter = keep.tile([P, 1], F32, name="quarter")
+        cos_rows = keep.tile([P, 1], F32, name="cos_rows")
         phase = keep.tile([P, 1], F32, name="phase")
         freq_row = keep.tile([P, 2, 8, 8], F32, name="freq_row")
         freq_diag = keep.tile([P, P], F32, name="freq_diag")
         freq = keep.tile([P, 1], F32, name="freq")
-        whole = keep.tile([P, S], I32, name="whole")
+        whole_turns = keep.tile([P, S], I32, name="whole_turns")
         rest = keep.tile([P, S], F32, name="rest")
-        trig_t = keep.tile([P, 4, P], F32, name="trig_t")
-        trig = psum.tile([P, 4, P], F32, name="trig")
+        trig_t = keep.tile([P, PACK, P], F32, name="trig_t")
+        trig = psum.tile([P, PACK, P], F32, name="trig")
 
-        V.memset(zero_one[:, 0:1], 0.0)
-        V.memset(zero_one[:, 1:2], 1.0)
-        make_identity(nc, ident[:])
-        nc.gpsimd.iota(
-            position[:], [[1, 4], [4, P]], base=0, channel_multiplier=0, allow_small_or_imprecise_dtypes=True
+        vector.memset(quarter[0:HALF, :], 0.25)
+        vector.memset(quarter[HALF:P, :], 0.0)
+        vector.memset(zero_one[:, 0:1], 0.0)
+        vector.memset(zero_one[:, 1:2], 1.0)
+        gpsimd.iota(
+            position[:], [[1, PACK], [PACK, P]], base=0, channel_multiplier=0, allow_small_or_imprecise_dtypes=True
         )
-        V.memset(quarter[0:HALF, :], 0.25)
-        V.memset(quarter[HALF:P, :], 0.0)
-        A.activation(out=warm[:], in_=zero_one[:, 0:1], func=ACT.Sin)
+        make_identity(nc, ident[:])
+        scalar.activation(out=cos_rows[:], in_=quarter[:], func=ACT.Sin, scale=2 * math.pi)
+        scalar.activation(out=phase[:], in_=cos_rows[:], func=ACT.Copy, scale=math.pi / 2)
         for a in range(0, 8, 2):
-            lo, hi = (THETA ** (-8 * e / HALF) / (2 * math.pi) for e in (a, a + 1))
-            V.tensor_scalar(
-                out=coarse[:, a : a + 2], in0=zero_one[:], scalar1=hi - lo, scalar2=lo, op0=ALU.mult, op1=ALU.add
-            )
-            lo, hi = (THETA ** (-e / HALF) for e in (a, a + 1))
-            V.tensor_scalar(
-                out=fine[:, a : a + 2], in0=zero_one[:], scalar1=hi - lo, scalar2=lo, op0=ALU.mult, op1=ALU.add
-            )
-        V.tensor_scalar(out=phase[:], in0=quarter[:], scalar1=2 * math.pi, scalar2=None, op0=ALU.mult)
-        V.tensor_tensor(
+            for tile, factor, stride in ((coarse, 1 / (2 * math.pi), 8), (fine, 1.0, 1)):
+                first, second = (factor * THETA ** (-stride * e / HALF) for e in (a, a + 1))
+                vector.tensor_scalar(
+                    out=tile[:, a : a + 2],
+                    in0=zero_one[:],
+                    scalar1=second - first,
+                    scalar2=first,
+                    op0=ALU.mult,
+                    op1=ALU.add,
+                )
+        vector.tensor_tensor(
             out=freq_row[:],
             in0=coarse[:].unsqueeze(1).unsqueeze(3).to_broadcast([P, 2, 8, 8]),
             in1=fine[:].unsqueeze(1).unsqueeze(1).to_broadcast([P, 2, 8, 8]),
             op=ALU.mult,
         )
-        V.scalar_tensor_tensor(
+        vector.scalar_tensor_tensor(
             out=freq_diag[:],
-            in0=freq_row[:].rearrange("p s a b -> p (s a b)"),
+            in0=freq_row[:].rearrange("p s a c -> p (s a c)"),
             scalar=1.0,
             in1=ident[:],
             op0=ALU.mult,
@@ -282,169 +348,187 @@ def tile_multiheadattention_pa_v_kernel(
             accum_out=freq[:],
         )
         flat_position = position[:].rearrange("p j r -> p (j r)")
-        V.tensor_scalar(
-            out=whole[:], in0=flat_position, scalar1=freq[:], scalar2=quarter[:], op0=ALU.mult, op1=ALU.add
+        vector.tensor_scalar(
+            out=whole_turns[:], in0=flat_position, scalar1=freq[:], scalar2=quarter[:], op0=ALU.mult, op1=ALU.add
         )
-        V.scalar_tensor_tensor(
-            out=rest[:], in0=flat_position, scalar=freq[:], in1=whole[:], op0=ALU.mult, op1=ALU.subtract
+        vector.scalar_tensor_tensor(
+            out=rest[:], in0=flat_position, scalar=freq[:], in1=whole_turns[:], op0=ALU.mult, op1=ALU.subtract
         )
-        A.activation(
+        scalar.activation(
             out=trig_t[:].rearrange("p j r -> p (j r)"), in_=rest[:], func=ACT.Sin, bias=phase[:], scale=2 * math.pi
         )
-        for j in range(4):
+        for j in range(PACK):
             nc.tensor.transpose(trig[:, j, :], trig_t[:, j, :], ident[:])
 
+        operands(x_op(0, 0))
+        operands(x_op(0, 1), x_op(1, 0))
+        operands(dz_tok(0, KV), dz_tok(1, KV))
+        interleave(vector, x_op(0, 0), x_raw[0, 0])
+        quantize((x_op(0, 0),), E4M3)
+        interleave(scalar, x_op(0, 1), x_raw[0, 1])
+        interleave(scalar, x_op(1, 0), x_raw[1, 0])
+        scalar.copy(out=dz_kv[:, :, :, KV_WIDTH:N].rearrange("p b j (h d) -> p b h j d", h=2), in_=v_raw[:])
+        products(0, KV, 0)
+        combine(gpsimd, 0, KV, 0)
+        products(0, KV, 1)
+        products(1, KV, 0)
+        combine(vector, 0, KV, 1)
+        combine(gpsimd, 1, KV, 0)
+        products(1, KV, 1)
+        interleave(scalar, dz_tok(0, KV), dz[0, KV])
+        multiply(COS, 0, Q_LO, 0)
+        combine(vector, 1, KV, 1)
+        interleave(scalar, dz_tok(1, KV), dz[1, KV])
+        turns(dz_feat(0, KV), dz[0, KV])
+        turns(w_op(KV, 0), w_raw[KV, 0])
+        turns(dz_feat(1, KV), dz[1, KV])
+        operands(dz_feat(0, KV), dz_feat(0, Q_LO))
+        operands(w_op(KV, 0), w_op(Q_LO, 0))
 
-        LO, HI = slice(0, 2), slice(2, 4)
+        multiply(SIN, 0, Q_LO, 1)
+        quantize((x_op(0, 1), x_op(1, 0)), E4M3)
+        combine(gpsimd, 0, Q_LO, 0)
+        turn_out(vector, dz_feat(0, KV), 0)
+        turn_out(scalar, dz_feat(0, KV), 1)
+        turns(w_op(Q_LO, 0), w_raw[Q_LO, 0])
+        turns_out(w_op(KV, 0))
+        turns(w_op(Q_HI, 0), w_raw[Q_HI, 0])
+        operands(dz_feat(1, KV), dz_feat(1, Q_LO))
+        turns_out(w_op(Q_LO, 0))
 
-        def turns(key, src):
-            turn(key, src, 0)
-            turn(key, src, 1)
+        products(0, Q_LO, 1)
+        quantize((dz_tok(0, KV), dz_tok(1, KV)), E5M2)
+        combine(gpsimd, 0, Q_LO, 1)
+        operands(w_op(Q_HI, 0), x_op(1, 1))
+        turn_out(vector, dz_feat(1, KV), 0)
+        turns_out(w_op(Q_HI, 0))
+        turn_out(scalar, dz_feat(1, KV), 1)
+        interleave(scalar, x_op(1, 1), x_raw[1, 1])
+        dw_matmuls(0, KV)
+        dw_matmuls(1, KV)
+        turns(w_op(KV, 1), w_raw[KV, 1])
+        dw_matmuls(2, KV)
+        turns(dz_feat(0, Q_LO), dz[0, Q_LO])
 
-        def turns_out(key, e0=A, e1=A):
-            turn_out(e0, key, 0)
-            turn_out(e1, key, 1)
+        products(0, Q_HI, 0)
+        quantize((w_op(KV, 0), w_op(Q_LO, 0)), E4M3)
+        combine(gpsimd, 0, Q_HI, 0)
+        dw_out(vector, 0, KV)
+        dw_out(scalar, 1, KV)
+        dw_out(scalar, 2, KV)
+        turns(w_op(Q_LO, 1), w_raw[Q_LO, 1])
+        dw_matmuls(3, KV)
+        turns_out(dz_feat(0, Q_LO))
+        operands(dz_tok(0, Q_LO), dz_tok(1, Q_LO))
+        interleave(scalar, dz_tok(0, Q_LO), dz[0, Q_LO], 0, 2)
+        operands(w_op(KV, 1), w_op(Q_LO, 1))
+        turns(w_op(Q_HI, 1), w_raw[Q_HI, 1])
+        dw_out(scalar, 3, KV)
 
-        def dw_mm(i, g):
-            dw_pass(i, g, 0)
-            dw_pass(i, g, 1)
-
-        def products(b, g, s, rows=slice(0, 4)):
-            multiply(COS, b, g, s, rows)
-            multiply(SIN, b, g, 1 - s, rows)
-
-        def dx_mm(b, j, n, passes):
-            for g in passes:
-                dx_pass(b, j, n, g, g == 2, g == 1)
-
-        operands("x00")
-        operands("x10")
-        operands("x01", "x11")
-        operands("zt02", "zt12")
-        interleave(V, "x00", x_raw[0, 0][:])
-        quantize(("x00",), E4M3)
-        interleave(A, "x10", x_raw[1, 0][:])
-        interleave(A, "x01", x_raw[0, 1][:])
-        products(0, 2, 0)
-        rotate(G, 0, 2, 0)
-        products(0, 2, 1)
-        quantize(("x10",), E4M3)
-        rotate(G, 0, 2, 1)
-        products(1, 2, 0)
-        rotate(G, 1, 2, 0)
-        products(1, 2, 1)
-        interleave(A, "zt02", dz[0, 2][:])
-        multiply(COS, 0, 0, 0)
-        rotate(V, 1, 2, 1)
-        interleave(A, "x11", x_raw[1, 1][:])
-        multiply(SIN, 0, 0, 1)
-        interleave(V, "zt12", dz[1, 2][:])
-        rotate(G, 0, 0, 0)
-        operands("w20", "w00")
-        turns("w20", w_raw[2, 0])
-        turns("zf02", dz[0, 2][:])
-        multiply(COS, 0, 0, 1)
-        multiply(SIN, 0, 0, 0)
-        quantize(("zt02", "zt12"), E5M2)
-        rotate(G, 0, 0, 1)
-        turns_out("w20")
-        turns("w00", w_raw[0, 0])
-        operands("zf02", "zf00")
-        turns_out("zf02")
-        for i in range(3):
-            dw_mm(i, 2)
-        turns_out("w00")
-        products(0, 1, 0)
-        quantize(("x01", "x11"), E4M3)
-        rotate(G, 0, 1, 0)
-        dw_mm(3, 2)
-        turns("w10", w_raw[1, 0])
-        for i in range(4):
-            dw_out(A, i, 2)
-        operands("w10", "w21")
-        turns("zf00", dz[0, 0][:])
-        turns_out("w10")
+        products(0, Q_HI, 1)
+        quantize((w_op(Q_HI, 0), x_op(1, 1)), E4M3)
+        combine(gpsimd, 0, Q_HI, 1)
+        turn_out(vector, w_op(KV, 1), 0)
+        turn_out(scalar, w_op(KV, 1), 1)
         for i in range(4, 7):
-            dw_mm(i, 2)
-        turns_out("zf00")
-        products(0, 1, 1)
-        quantize(("w20", "w00"), E4M3)
-        rotate(G, 0, 1, 1)
-        dw_mm(7, 2)
-        turns("w21", w_raw[2, 1])
-        for i in range(4, 8):
-            dw_out(A, i, 2)
-        turns("w01", w_raw[0, 1])
-        turns_out("w21")
-        products(1, 0, 0)
-        quantize(("zf02", "zf00"), E5M2)
-        rotate(G, 1, 0, 0)
-        operands("w01", "w11")
-        turns("zf01", dz[0, 1][:])
-        turns_out("w01")
-        turns("w11", w_raw[1, 1])
-        operands("zf01")
-        turns_out("zf01")
+            dw_matmuls(i, KV)
+        turns_out(w_op(Q_LO, 1))
+        operands(w_op(Q_HI, 1))
+        turns_out(w_op(Q_HI, 1))
+        dw_matmuls(7, KV)
+        turns(dz_feat(0, Q_HI), dz[0, Q_HI])
+
+        products(1, Q_LO, 0)
+        quantize((dz_feat(0, KV), dz_feat(0, Q_LO)), E5M2)
+        combine(gpsimd, 1, Q_LO, 0)
+        dw_out(vector, 4, KV)
+        dw_out(scalar, 5, KV)
+        operands(dz_tok(0, Q_HI))
+        interleave(scalar, dz_tok(0, Q_HI), dz[0, Q_HI], 0, 2)
+        operands(dz_feat(0, Q_HI))
         for j in range(3):
-            dx_mm(0, j, 0, (2, 0))
-        turns_out("w11")
-        products(1, 0, 1)
-        quantize(("w10", "w21"), E4M3)
-        quantize(("zf01",), E5M2)
-        operands("zt00", "zt10")
-        interleave(A, "zt00", dz[0, 0][:])
-        dx_mm(0, 3, 0, (2, 0))
-        for j in range(4):
-            dx_mm(0, j, 0, (1,))
-        rotate(V, 1, 0, 1)
-        quantize(("w01", "w11"), E4M3)
-        interleave(V, "zt10", dz[1, 0][:])
-        turns("zf12", dz[1, 2][:])
-        for j in range(4):
-            dx_out(A, 0, j, 0)
-        operands("zf12", "zf10")
-        for j in range(2):
-            dx_mm(0, j, 1, (2, 0, 1))
-        turns_out("zf12")
-        turns("zf10", dz[1, 0][:])
-        multiply(COS, 1, 1, 0)
-        quantize(("zt00", "zt10"), E5M2)
-        for j in range(2, 4):
-            dx_mm(0, j, 1, (2, 0, 1))
-        for j in range(2):
-            dx_out(A, 0, j, 1)
-        turns_out("zf10")
-        for j in range(2, 4):
-            dx_out(A, 0, j, 1)
-        multiply(SIN, 1, 1, 1)
-        rotate(G, 1, 1, 0)
-        operands("zt01", "zt11")
-        operands("zf11")
-        for i in range(4):
-            dw_mm(i, 0)
-        products(1, 1, 1)
-        quantize(("zf12", "zf10"), E5M2)
-        interleave(A, "zt01", dz[0, 1][:])
-        rotate(V, 1, 1, 1, LO)
-        rotate(V, 1, 1, 1, HI)
-        for i in range(4):
-            dw_out(A, i, 0)
-        for i in range(4, 6):
-            dw_mm(i, 0)
-        turns("zf11", dz[1, 1][:])
-        for i in range(6, 8):
-            dw_mm(i, 0)
-        interleave(V, "zt11", dz[1, 1][:])
-        turn_out(V, "zf11", 0)
-        turn_out(A, "zf11", 1)
-        for i in range(4, 8):
-            dw_out(A, i, 0)
-        quantize(("zt01", "zt11"), E5M2)
-        quantize(("zf11",), E5M2)
-        for j in range(4):
-            for n in range(2):
-                dx_mm(1, j, n, (2, 0, 1))
-                dx_out((A, V)[n], 1, j, n)
+            dx_matmuls(0, j, 0, (KV, Q_LO))
+        turns_out(dz_feat(0, Q_HI))
+        dw_out(scalar, 6, KV)
+        dw_out(scalar, 7, KV)
+        dx_matmuls(0, 3, 0, (KV, Q_LO))
+        interleave(scalar, dz_tok(0, Q_LO), dz[0, Q_LO], 1, 2)
+
+        products(1, Q_LO, 1)
+        quantize((dz_feat(0, Q_HI),), E5M2)
+        quantize((w_op(KV, 1), w_op(Q_LO, 1)), E4M3)
+        combine(vector, 1, Q_LO, 1)
+        quantize((w_op(Q_HI, 1),), E4M3)
+        interleave(vector, dz_tok(1, Q_LO), dz[1, Q_LO])
+        for j in range(PACK):
+            dx_matmuls(0, j, 0, (Q_HI,))
+        for j in range(3):
+            dx_matmuls(0, j, 1, (KV, Q_LO))
+        for j in range(PACK):
+            dx_out(scalar, 0, j, 0)
+        interleave(scalar, dz_tok(0, Q_HI), dz[0, Q_HI], 1, 2)
+        turn(dz_feat(1, Q_LO), dz[1, Q_LO], 0)
+        for j in range(3):
+            dx_matmuls(0, j, 1, (Q_HI,))
+        turn(dz_feat(1, Q_LO), dz[1, Q_LO], 1)
+        multiply(COS, 1, Q_HI, 0, FIRST_ROWS)
+        quantize((dz_tok(0, Q_LO), dz_tok(1, Q_LO)), E5M2)
+        dx_matmuls(0, 3, 1)
+        dx_out(scalar, 0, 0, 1)
+        dx_out(scalar, 0, 1, 1)
+        turns_out(dz_feat(1, Q_LO))
+
+        multiply(SIN, 1, Q_HI, 1, FIRST_ROWS)
+        combine(gpsimd, 1, Q_HI, 0, FIRST_ROWS)
+        products(1, Q_HI, 1, FIRST_ROWS)
+        multiply(COS, 1, Q_HI, 0, LAST_ROWS)
+        multiply(COS, 1, Q_HI, 1, LAST_ROWS)
+        combine(vector, 1, Q_HI, 1, FIRST_ROWS)
+        multiply(SIN, 1, Q_HI, 0, LAST_ROWS)
+        quantize((dz_feat(1, KV), dz_feat(1, Q_LO)), E5M2)
+        for i in range(3):
+            dw_matmuls(i, Q_LO)
+        dx_out(scalar, 0, 2, 1)
+        dx_out(scalar, 0, 3, 1)
+        operands(dz_feat(1, Q_HI))
+        dw_matmuls(3, Q_LO)
+        dw_matmuls(4, Q_LO)
+        dw_out(scalar, 0, Q_LO)
+        dw_matmuls(5, Q_LO)
+        dw_out(scalar, 1, Q_LO)
+        dw_out(scalar, 2, Q_LO)
+        turn(dz_feat(1, Q_HI), dz[1, Q_HI], 0)
+        dw_out(scalar, 3, Q_LO)
+        dw_matmuls(6, Q_LO)
+        dw_out(scalar, 4, Q_LO)
+        turn_out(scalar, dz_feat(1, Q_HI), 0)
+        dw_matmuls(7, Q_LO)
+        multiply(SIN, 1, Q_HI, 1, LAST_ROWS)
+        quantize((dz_feat(1, Q_HI),), E5M2, 0, 2)
+        combine(vector, 1, Q_HI, 1, LAST_ROWS)
+        combine(vector, 1, Q_HI, 0, LAST_ROWS)
+        quantize((dz_tok(0, Q_HI),), E5M2)
+        for i in range(5, 8):
+            dw_out(scalar, i, Q_LO)
+        for n in range(2):
+            dx_matmuls(1, 0, n)
+        turn(dz_feat(1, Q_HI), dz[1, Q_HI], 1)
+        operands(dz_tok(1, Q_HI))
+        interleave(vector, dz_tok(1, Q_HI), dz[1, Q_HI])
+        for n in range(2):
+            dx_out(scalar, 1, 0, n, whole_rows=True)
+        turn_out(scalar, dz_feat(1, Q_HI), 1)
+        for n in range(2):
+            dx_matmuls(1, 1, n)
+        quantize((dz_tok(1, Q_HI),), E5M2)
+        quantize((dz_feat(1, Q_HI),), E5M2, 1, 2)
+        for n in range(2):
+            dx_out(scalar, 1, 1, n)
+
         for i in range(8):
-            dw_mm(i, 1)
-            dw_out((A, V)[i % 2], i, 1)
+            dw_matmuls(i, Q_HI)
+            dw_out((vector, scalar)[i % 2], i, Q_HI)
+        for j in range(LAST_ROWS.start, LAST_ROWS.stop):
+            for n in range(2):
+                dx_matmuls(1, j, n)
+                dx_out((vector, scalar)[n], 1, j, n, whole_rows=j < PACK - 1)

import math
from contextlib import ExitStack

import concourse.mybir as mybir
from concourse.masks import make_identity

F32 = mybir.dt.float32
BF16 = mybir.dt.bfloat16
I32 = mybir.dt.int32
U32 = mybir.dt.uint32
U8 = mybir.dt.uint8
E4M3 = mybir.dt.float8_e4m3fn_x4
E5M2 = mybir.dt.float8_e5m2_x4
ALU = mybir.AluOpType
ACT = mybir.ActivationFunctionType

P = 128
B, S, HID, D = 2, 512, 1024, 128
KV_WIDTH = 256
HALF = D // 2
THETA = 10000.0
N = 512
PACK = 4
Q_LO, Q_HI, KV = 0, 1, 2
COS, SIN = 0, 1
ALL_ROWS, FIRST_ROWS, LAST_ROWS = slice(0, 4), slice(0, 2), slice(2, 4)

WORK_BANKS = 7
SINGLE_SLOTS, PAIR_SLOTS = 3, 5
PRODUCT_BUFS = 9
BANK_STAGING_BUFS = 5
DZ_PLACE = {(0, Q_LO): "v_raw", (0, Q_HI): "k_raw", (1, Q_LO): "wkv_0", (1, Q_HI): "q_0_0"}
TWO_BANK_STAGING_PLACES = ("x_0", "x_1", "wkv_1", "q_0_1", "wq_0", "wq_1")

FLOPS = 2 * 2 * (B * S) * HID * (HID + 2 * KV_WIDTH)


def x_op(b, n):
    return f"x{b}{n}"


def w_op(g, n):
    return f"w{g}{n}"


def dz_tok(b, g):
    return f"zt{b}{g}"


def dz_feat(b, g):
    return f"zf{b}{g}"


def tile_multiheadattention_pa_v_kernel(
    tc, hidden_states, wq, wk, wv, grad_0, grad_1, grad_2, out_0, out_1, out_2, out_3
):
    nc = tc.nc
    vector, scalar, gpsimd = nc.vector, nc.scalar, nc.gpsimd
    with ExitStack() as ctx:
        keep = ctx.enter_context(tc.tile_pool(name="keep", bufs=1))
        work = ctx.enter_context(tc.tile_pool(name="work", bufs=1))
        psum = ctx.enter_context(tc.psum_pool(name="psum", bufs=1))
        ctx.enter_context(tc.manual_schedule())

        x_raw, w_raw, grad_raw, dz, product = {}, {}, {}, {}, {}
        grouped, codes, scales, together, slot_of = {}, {}, {}, {}, {}
        banks, bank_number, staged = {}, {}, {}
        free_banks = list(range(WORK_BANKS))
        free_slots = {1: list(range(SINGLE_SLOTS)), 2: list(range(PAIR_SLOTS))}
        staging_places = list(TWO_BANK_STAGING_PLACES)


        def take_bank(key, shape):
            bank_number[key] = free_banks[0]
            free_banks.remove(bank_number[key])
            banks[key] = psum.tile(shape, F32, name=f"bank_{key}", tag=f"bank{bank_number[key]}")
            return banks[key]

        def give_bank(key):
            free_banks.append(bank_number[key])

        def next_staging_place():
            place = staging_places[0]
            staging_places.remove(place)
            staging_places.append(place)
            return place

        def copy_on(engine, out, in_):
            if engine is scalar:
                scalar.copy(out=out, in_=in_)
            else:
                vector.tensor_copy(out=out, in_=in_)


        def load_x(b):
            tile = keep.tile([P, PACK, HID], BF16, name=f"x_raw_{b}", tag=f"x_{b}")
            nc.sync.dma_start(out=tile[:], in_=hidden_states[b].rearrange("(p j) c -> p j c", j=PACK))
            for n in range(2):
                x_raw[b, n] = tile[:, :, n * N : (n + 1) * N]

        def load_q(b, g):
            tile = keep.tile([P, 4, PACK, D], BF16, name=f"q_raw_{b}_{g}", tag=f"q_{b}_{g}")
            heads = grad_0[b, 4 * g : 4 * g + 4]
            nc.sync.dma_start(out=tile[:], in_=heads.rearrange("h (p j) d -> p h j d", j=PACK))
            grad_raw[b, g] = tile[:]

        def load_two_heads(grad, name):
            tile = keep.tile([P, B, 2, PACK, D], BF16, name=name, tag=name)
            nc.sync.dma_start(
                out=tile[:].rearrange("p b h j d -> p (b h) (j d)"),
                in_=grad.rearrange("b h (p j) d -> p (b h) (j d)", j=PACK),
            )
            return tile

        def load_wq(n):
            tile = keep.tile([P, 4, HID], BF16, name=f"wq_raw_{n}", tag=f"wq_{n}")
            nc.sync.dma_start(out=tile[:], in_=wq[n * N : (n + 1) * N, :].rearrange("(i p) k -> p i k", p=P))
            w_raw[Q_LO, n] = tile[:, :, 0:N]
            w_raw[Q_HI, n] = tile[:, :, N:HID]

        def load_wkv(n):
            tile = keep.tile([P, 4, N], BF16, name=f"wkv_raw_{n}", tag=f"wkv_{n}")
            rows = slice(n * N, (n + 1) * N)
            nc.sync.dma_start(out=tile[:, :, 0:KV_WIDTH], in_=wk[rows, :].rearrange("(i p) k -> p i k", p=P))
            nc.sync.dma_start(out=tile[:, :, KV_WIDTH:N], in_=wv[rows, :].rearrange("(i p) k -> p i k", p=P))
            w_raw[KV, n] = tile[:]


        def operands(*keys):
            name = "_".join(keys)
            width = N * len(keys)
            slot_of[keys] = free_slots[len(keys)][0]
            free_slots[len(keys)].remove(slot_of[keys])
            tag = f"grouped_{len(keys)}_{slot_of[keys]}"
            together[keys] = (
                work.tile([P, width, PACK], BF16, name=f"grouped_{name}", tag=tag, align_bytes=64),
                keep.tile([P, width], U32, name=f"code_{name}", align_bytes=64),
                keep.tile([P, width], U8, name=f"scale_{name}", align_bytes=64),
            )
            for k, key in enumerate(keys):
                cols = slice(k * N, (k + 1) * N)
                grouped[key] = together[keys][0][:, cols, :]
                codes[key] = together[keys][1][:, cols]
                scales[key] = together[keys][2][:, cols]

        def quantize(keys, fmt, part=0, parts=1):
            values, code, scale = together[keys]
            width = N * len(keys) // parts
            cols = slice(part * width, (part + 1) * width)
            vector.quantize_mx(
                out=code[:, cols].bitcast(fmt),
                scales=scale[:, cols],
                in_=values[:, cols, :].rearrange("p c j -> p (c j)"),
            )
            if part == parts - 1:
                free_slots[len(keys)].append(slot_of[keys])

        def interleave(engine, key, src, part=0, parts=1):
            cols = slice(part * N // parts, (part + 1) * N // parts)
            copy_on(
                engine,
                grouped[key][:, cols, :].rearrange("p (c i) j -> p c j i", i=4),
                src[:, :, cols].rearrange("p j (c i) -> p c j i", i=4),
            )

        def turn(key, src, pair):
            bank = take_bank(f"{key}_{pair}", [P, 2, 2, P])
            words = src.bitcast(F32)
            for r in range(2):
                for u in range(2):
                    nc.tensor.transpose(bank[:, r, u, :], words[:, 2 * pair + r, u : N // 2 : 2], ident[:])

        def turn_out(engine, key, pair):
            words = grouped[key].rearrange("p c t -> p (c t)").bitcast(F32)
            copy_on(
                engine,
                words[:, pair * N : (pair + 1) * N].rearrange("p (r c u) -> p r c u", r=2, u=2),
                banks[f"{key}_{pair}"][:].rearrange("p r u c -> p r c u"),
            )
            give_bank(f"{key}_{pair}")

        def turns(key, src):
            for pair in range(2):
                turn(key, src, pair)

        def turns_out(key):
            for pair in range(2):
                turn_out(scalar, key, pair)


        def multiply(which, b, g, half, rows=ALL_ROWS):
            heads = grad_raw[b, g].shape[1]
            if rows.start == 0:
                product[which, b, g, half] = work.tile(
                    [P, heads, PACK, HALF],
                    F32,
                    name=f"prod_{which}_{b}_{g}_{half}",
                    tag="product",
                    bufs=PRODUCT_BUFS,
                )
            table = trig[:, rows, which * HALF : (which + 1) * HALF]
            vector.tensor_tensor(
                out=product[which, b, g, half][:, :, rows],
                in0=grad_raw[b, g][:, :, rows, half * HALF : (half + 1) * HALF],
                in1=table.unsqueeze(1).to_broadcast([P, heads, rows.stop - rows.start, HALF]),
                op=ALU.mult,
            )

        def products(b, g, half, rows=ALL_ROWS):
            multiply(COS, b, g, half, rows)
            multiply(SIN, b, g, 1 - half, rows)

        def combine(engine, b, g, half, rows=ALL_ROWS):
            heads = grad_raw[b, g].shape[1]
            if (b, g) not in dz:
                tile = keep.tile([P, PACK, N], BF16, name=f"dz_{b}_{g}", tag=DZ_PLACE[b, g])
                dz[b, g] = tile[:]
            engine.tensor_tensor(
                out=dz[b, g].rearrange("p j (h s d) -> p s h j d", s=2, d=HALF)[:, half, 0:heads, rows],
                in0=product[COS, b, g, half][:, :, rows],
                in1=product[SIN, b, g, 1 - half][:, :, rows],
                op=ALU.add if half == 0 else ALU.subtract,
            )


        def matmul(acc, lhs, m, rhs, start, stop, lhs_fmt, rhs_fmt):
            cols = slice(m * P, (m + 1) * P)
            nc.tensor.matmul_mx(
                out=acc[:],
                lhsT=codes[lhs][:, cols].bitcast(lhs_fmt),
                lhsT_scale=scales[lhs][:, cols],
                rhs=codes[rhs].bitcast(rhs_fmt),
                rhs_scale=scales[rhs],
                start=start,
                stop=stop,
            )

        def dx_matmuls(b, j, n, groups=(KV, Q_LO, Q_HI)):
            key = f"dx{b}{j}{n}"
            for g in groups:
                if g == KV:
                    take_bank(key, [P, N])
                matmul(banks[key], dz_feat(b, g), j, w_op(g, n), g == KV, g == Q_HI, E5M2, E4M3)

        def dx_out(engine, b, j, n, whole_rows=False):
            key = f"dx{b}{j}{n}"
            rows = out_0[b].rearrange("(p j) c -> p j c", j=PACK)[:, j, :]
            cols = slice(n * N, (n + 1) * N)
            if not whole_rows:
                tile = work.tile([P, N], F32, name=f"dx_rows_{b}_{j}_{n}", tag="staged", bufs=BANK_STAGING_BUFS)
                copy_on(engine, tile[:], banks[key][:])
                nc.sync.dma_start(out=rows[:, cols], in_=tile[:])
            else:
                if n == 0:
                    staged["dx"] = keep.tile([P, HID], F32, name=f"dx_rows_{b}_{j}", tag=next_staging_place())
                copy_on(engine, staged["dx"][:, cols], banks[key][:])
                if n == 1:
                    nc.sync.dma_start(out=rows, in_=staged["dx"][:])
            give_bank(key)

        def dw_matmuls(i, g):
            acc = take_bank(f"dw{i}{g}", [P, N])
            for b in range(B):
                matmul(acc, x_op(b, i // 4), i % 4, dz_tok(b, g), b == 0, b == B - 1, E4M3, E5M2)

        def dw_out(engine, i, g):
            if i % 2 == 0:
                staged["dw"] = keep.tile([P, 2, N], F32, name=f"dw_rows_{i}_{g}", tag=next_staging_place())
            tile = staged["dw"]
            copy_on(engine, tile[:, i % 2, :], banks[f"dw{i}{g}"][:])
            give_bank(f"dw{i}{g}")
            if i % 2 == 1:
                rows = slice((i - 1) * P, (i + 1) * P)
                if g == KV:
                    for out, cols in ((out_2, slice(0, KV_WIDTH)), (out_3, slice(KV_WIDTH, N))):
                        nc.sync.dma_start(out=out[rows, :].rearrange("(i p) c -> p i c", p=P), in_=tile[:, :, cols])
                else:
                    dest = out_1[rows, g * N : (g + 1) * N]
                    nc.sync.dma_start(out=dest.rearrange("(i p) c -> p i c", p=P), in_=tile[:])

        load_x(0)
        k_raw = load_two_heads(grad_1, "k_raw")
        load_x(1)
        v_raw = load_two_heads(grad_2, "v_raw")
        load_q(0, Q_LO)
        load_wkv(0)
        load_wq(0)
        load_q(0, Q_HI)
        load_wkv(1)
        load_wq(1)
        load_q(1, Q_LO)
        load_q(1, Q_HI)
        dz_kv = keep.tile([P, B, PACK, N], BF16, name="dz_kv")
        for b in range(B):
            grad_raw[b, KV] = k_raw[:, b]
            dz[b, KV] = dz_kv[:, b]

        zero_one = keep.tile([P, 2], F32, name="zero_one")
        ident = keep.tile([P, P], F32, name="ident")
        position = keep.tile([P, PACK, P], F32, name="position")
        coarse = keep.tile([P, 8], F32, name="coarse")
        fine = keep.tile([P, 8], F32, name="fine")
        quarter = keep.tile([P, 1], F32, name="quarter")
        cos_rows = keep.tile([P, 1], F32, name="cos_rows")
        phase = keep.tile([P, 1], F32, name="phase")
        freq_row = keep.tile([P, 2, 8, 8], F32, name="freq_row")
        freq_diag = keep.tile([P, P], F32, name="freq_diag")
        freq = keep.tile([P, 1], F32, name="freq")
        whole_turns = keep.tile([P, S], I32, name="whole_turns")
        rest = keep.tile([P, S], F32, name="rest")
        trig_t = keep.tile([P, PACK, P], F32, name="trig_t")
        trig = psum.tile([P, PACK, P], F32, name="trig")

        vector.memset(quarter[0:HALF, :], 0.25)
        vector.memset(quarter[HALF:P, :], 0.0)
        vector.memset(zero_one[:, 0:1], 0.0)
        vector.memset(zero_one[:, 1:2], 1.0)
        gpsimd.iota(
            position[:], [[1, PACK], [PACK, P]], base=0, channel_multiplier=0, allow_small_or_imprecise_dtypes=True
        )
        make_identity(nc, ident[:])
        scalar.activation(out=cos_rows[:], in_=quarter[:], func=ACT.Sin, scale=2 * math.pi)
        scalar.activation(out=phase[:], in_=cos_rows[:], func=ACT.Copy, scale=math.pi / 2)
        for a in range(0, 8, 2):
            for tile, factor, stride in ((coarse, 1 / (2 * math.pi), 8), (fine, 1.0, 1)):
                first, second = (factor * THETA ** (-stride * e / HALF) for e in (a, a + 1))
                vector.tensor_scalar(
                    out=tile[:, a : a + 2],
                    in0=zero_one[:],
                    scalar1=second - first,
                    scalar2=first,
                    op0=ALU.mult,
                    op1=ALU.add,
                )
        vector.tensor_tensor(
            out=freq_row[:],
            in0=coarse[:].unsqueeze(1).unsqueeze(3).to_broadcast([P, 2, 8, 8]),
            in1=fine[:].unsqueeze(1).unsqueeze(1).to_broadcast([P, 2, 8, 8]),
            op=ALU.mult,
        )
        vector.scalar_tensor_tensor(
            out=freq_diag[:],
            in0=freq_row[:].rearrange("p s a c -> p (s a c)"),
            scalar=1.0,
            in1=ident[:],
            op0=ALU.mult,
            op1=ALU.mult,
            accum_out=freq[:],
        )
        flat_position = position[:].rearrange("p j r -> p (j r)")
        vector.tensor_scalar(
            out=whole_turns[:], in0=flat_position, scalar1=freq[:], scalar2=quarter[:], op0=ALU.mult, op1=ALU.add
        )
        vector.scalar_tensor_tensor(
            out=rest[:], in0=flat_position, scalar=freq[:], in1=whole_turns[:], op0=ALU.mult, op1=ALU.subtract
        )
        scalar.activation(
            out=trig_t[:].rearrange("p j r -> p (j r)"), in_=rest[:], func=ACT.Sin, bias=phase[:], scale=2 * math.pi
        )
        for j in range(PACK):
            nc.tensor.transpose(trig[:, j, :], trig_t[:, j, :], ident[:])

        operands(x_op(0, 0))
        operands(x_op(0, 1), x_op(1, 0))
        operands(dz_tok(0, KV), dz_tok(1, KV))
        interleave(vector, x_op(0, 0), x_raw[0, 0])
        quantize((x_op(0, 0),), E4M3)
        interleave(scalar, x_op(0, 1), x_raw[0, 1])
        interleave(scalar, x_op(1, 0), x_raw[1, 0])
        scalar.copy(out=dz_kv[:, :, :, KV_WIDTH:N].rearrange("p b j (h d) -> p b h j d", h=2), in_=v_raw[:])
        products(0, KV, 0)
        combine(gpsimd, 0, KV, 0)
        products(0, KV, 1)
        products(1, KV, 0)
        combine(vector, 0, KV, 1)
        combine(gpsimd, 1, KV, 0)
        products(1, KV, 1)
        interleave(scalar, dz_tok(0, KV), dz[0, KV])
        multiply(COS, 0, Q_LO, 0)
        combine(vector, 1, KV, 1)
        interleave(scalar, dz_tok(1, KV), dz[1, KV])
        turns(dz_feat(0, KV), dz[0, KV])
        turns(w_op(KV, 0), w_raw[KV, 0])
        turns(dz_feat(1, KV), dz[1, KV])
        operands(dz_feat(0, KV), dz_feat(0, Q_LO))
        operands(w_op(KV, 0), w_op(Q_LO, 0))

        multiply(SIN, 0, Q_LO, 1)
        quantize((x_op(0, 1), x_op(1, 0)), E4M3)
        combine(gpsimd, 0, Q_LO, 0)
        turn_out(vector, dz_feat(0, KV), 0)
        turn_out(scalar, dz_feat(0, KV), 1)
        turns(w_op(Q_LO, 0), w_raw[Q_LO, 0])
        turns_out(w_op(KV, 0))
        turns(w_op(Q_HI, 0), w_raw[Q_HI, 0])
        operands(dz_feat(1, KV), dz_feat(1, Q_LO))
        turns_out(w_op(Q_LO, 0))

        products(0, Q_LO, 1)
        quantize((dz_tok(0, KV), dz_tok(1, KV)), E5M2)
        combine(gpsimd, 0, Q_LO, 1)
        operands(w_op(Q_HI, 0), x_op(1, 1))
        turn_out(vector, dz_feat(1, KV), 0)
        turns_out(w_op(Q_HI, 0))
        turn_out(scalar, dz_feat(1, KV), 1)
        interleave(scalar, x_op(1, 1), x_raw[1, 1])
        dw_matmuls(0, KV)
        dw_matmuls(1, KV)
        turns(w_op(KV, 1), w_raw[KV, 1])
        dw_matmuls(2, KV)
        turns(dz_feat(0, Q_LO), dz[0, Q_LO])

        products(0, Q_HI, 0)
        quantize((w_op(KV, 0), w_op(Q_LO, 0)), E4M3)
        combine(gpsimd, 0, Q_HI, 0)
        dw_out(vector, 0, KV)
        dw_out(scalar, 1, KV)
        dw_out(scalar, 2, KV)
        turns(w_op(Q_LO, 1), w_raw[Q_LO, 1])
        dw_matmuls(3, KV)
        turns_out(dz_feat(0, Q_LO))
        operands(dz_tok(0, Q_LO), dz_tok(1, Q_LO))
        interleave(scalar, dz_tok(0, Q_LO), dz[0, Q_LO], 0, 2)
        operands(w_op(KV, 1), w_op(Q_LO, 1))
        turns(w_op(Q_HI, 1), w_raw[Q_HI, 1])
        dw_out(scalar, 3, KV)

        products(0, Q_HI, 1)
        quantize((w_op(Q_HI, 0), x_op(1, 1)), E4M3)
        combine(gpsimd, 0, Q_HI, 1)
        turn_out(vector, w_op(KV, 1), 0)
        turn_out(scalar, w_op(KV, 1), 1)
        for i in range(4, 7):
            dw_matmuls(i, KV)
        turns_out(w_op(Q_LO, 1))
        operands(w_op(Q_HI, 1))
        turns_out(w_op(Q_HI, 1))
        dw_matmuls(7, KV)
        turns(dz_feat(0, Q_HI), dz[0, Q_HI])

        products(1, Q_LO, 0)
        quantize((dz_feat(0, KV), dz_feat(0, Q_LO)), E5M2)
        combine(gpsimd, 1, Q_LO, 0)
        dw_out(vector, 4, KV)
        dw_out(scalar, 5, KV)
        operands(dz_tok(0, Q_HI))
        interleave(scalar, dz_tok(0, Q_HI), dz[0, Q_HI], 0, 2)
        operands(dz_feat(0, Q_HI))
        for j in range(3):
            dx_matmuls(0, j, 0, (KV, Q_LO))
        turns_out(dz_feat(0, Q_HI))
        dw_out(scalar, 6, KV)
        dw_out(scalar, 7, KV)
        dx_matmuls(0, 3, 0, (KV, Q_LO))
        interleave(scalar, dz_tok(0, Q_LO), dz[0, Q_LO], 1, 2)

        products(1, Q_LO, 1)
        quantize((dz_feat(0, Q_HI),), E5M2)
        quantize((w_op(KV, 1), w_op(Q_LO, 1)), E4M3)
        combine(vector, 1, Q_LO, 1)
        quantize((w_op(Q_HI, 1),), E4M3)
        interleave(vector, dz_tok(1, Q_LO), dz[1, Q_LO])
        for j in range(PACK):
            dx_matmuls(0, j, 0, (Q_HI,))
        for j in range(3):
            dx_matmuls(0, j, 1, (KV, Q_LO))
        for j in range(PACK):
            dx_out(scalar, 0, j, 0)
        interleave(scalar, dz_tok(0, Q_HI), dz[0, Q_HI], 1, 2)
        turn(dz_feat(1, Q_LO), dz[1, Q_LO], 0)
        for j in range(3):
            dx_matmuls(0, j, 1, (Q_HI,))
        turn(dz_feat(1, Q_LO), dz[1, Q_LO], 1)
        multiply(COS, 1, Q_HI, 0, FIRST_ROWS)
        quantize((dz_tok(0, Q_LO), dz_tok(1, Q_LO)), E5M2)
        dx_matmuls(0, 3, 1)
        dx_out(scalar, 0, 0, 1)
        dx_out(scalar, 0, 1, 1)
        turns_out(dz_feat(1, Q_LO))

        multiply(SIN, 1, Q_HI, 1, FIRST_ROWS)
        combine(gpsimd, 1, Q_HI, 0, FIRST_ROWS)
        products(1, Q_HI, 1, FIRST_ROWS)
        multiply(COS, 1, Q_HI, 0, LAST_ROWS)
        multiply(COS, 1, Q_HI, 1, LAST_ROWS)
        combine(vector, 1, Q_HI, 1, FIRST_ROWS)
        multiply(SIN, 1, Q_HI, 0, LAST_ROWS)
        quantize((dz_feat(1, KV), dz_feat(1, Q_LO)), E5M2)
        for i in range(3):
            dw_matmuls(i, Q_LO)
        dx_out(scalar, 0, 2, 1)
        dx_out(scalar, 0, 3, 1)
        operands(dz_feat(1, Q_HI))
        dw_matmuls(3, Q_LO)
        dw_matmuls(4, Q_LO)
        dw_out(scalar, 0, Q_LO)
        dw_matmuls(5, Q_LO)
        dw_out(scalar, 1, Q_LO)
        dw_out(scalar, 2, Q_LO)
        turn(dz_feat(1, Q_HI), dz[1, Q_HI], 0)
        dw_out(scalar, 3, Q_LO)
        dw_matmuls(6, Q_LO)
        dw_out(scalar, 4, Q_LO)
        turn_out(scalar, dz_feat(1, Q_HI), 0)
        dw_matmuls(7, Q_LO)
        multiply(SIN, 1, Q_HI, 1, LAST_ROWS)
        quantize((dz_feat(1, Q_HI),), E5M2, 0, 2)
        combine(vector, 1, Q_HI, 1, LAST_ROWS)
        combine(vector, 1, Q_HI, 0, LAST_ROWS)
        quantize((dz_tok(0, Q_HI),), E5M2)
        for i in range(5, 8):
            dw_out(scalar, i, Q_LO)
        for n in range(2):
            dx_matmuls(1, 0, n)
        turn(dz_feat(1, Q_HI), dz[1, Q_HI], 1)
        operands(dz_tok(1, Q_HI))
        interleave(vector, dz_tok(1, Q_HI), dz[1, Q_HI])
        for n in range(2):
            dx_out(scalar, 1, 0, n, whole_rows=True)
        turn_out(scalar, dz_feat(1, Q_HI), 1)
        for n in range(2):
            dx_matmuls(1, 1, n)
        quantize((dz_tok(1, Q_HI),), E5M2)
        quantize((dz_feat(1, Q_HI),), E5M2, 1, 2)
        for n in range(2):
            dx_out(scalar, 1, 1, n)

        for i in range(8):
            dw_matmuls(i, Q_HI)
            dw_out((vector, scalar)[i % 2], i, Q_HI)
        for j in range(LAST_ROWS.start, LAST_ROWS.stop):
            for n in range(2):
                dx_matmuls(1, j, n)
                dx_out((vector, scalar)[n], 1, j, n, whole_rows=j < PACK - 1)
